import numpy as np
import ml_dtypes


def mxq(x, axis, fmt="e4m3"):
    dtype, down = {"e4m3": (ml_dtypes.float8_e4m3fn, 7), "e5m2": (ml_dtypes.float8_e5m2, 14)}[fmt]
    v = np.moveaxis(np.asarray(x, np.float32).astype(ml_dtypes.bfloat16).astype(np.float64), axis, -1)
    blocks = v.reshape(v.shape[:-1] + (-1, 32))
    amax = np.abs(blocks).max(-1, keepdims=True)
    byte = np.maximum(np.where(amax > 0, np.frexp(amax)[1] - 1 + 127, 0) - down, 1)
    scale = np.exp2(byte - 127.0)
    codes = (blocks / scale).astype(np.float32).astype(dtype).astype(np.float64)
    return np.moveaxis((codes * scale).reshape(v.shape), -1, axis)


WIDE = False


def mx_kscale(k):
    if not WIDE:
        return np.ones(k)
    levels = np.array([10, -10, 5, -5, 0])
    if k % 512:
        return np.exp2(np.random.permutation(np.resize(levels, k // 32))).repeat(32)
    a = np.empty((k // 512, 16))
    for p in range(k // 512):
        a[p, :8] = np.random.permutation(np.resize(levels, 8))
        for g in range(8):
            far = levels[np.abs(levels - a[p, g]) >= 10]
            a[p, g + 8] = far[np.random.randint(len(far))]
    return np.exp2(a.ravel()).repeat(32)


BF16 = ml_dtypes.bfloat16


def bf(x):
    return np.asarray(x, np.float32).astype(BF16)


def f64(x):
    return np.asarray(x).astype(np.float64)


B, N, DIM, H, DK, DV, KB = 8, 1024, 512, 2, 16, 48, 512
WT = 256.0
EPS = 1e-12
DI = H * (DK + DV)


def l2norm(t):
    n = np.sqrt((t * t).sum(-1, keepdims=True))
    return t / np.maximum(n, EPS)


def setup_inputs():
    s = mx_kscale(DIM)
    return {'tokens': bf(np.random.standard_normal((B, N, DIM)) * s),
            'w_qg': bf(np.random.standard_normal((DI, DIM)) / np.sqrt(DIM) / s[None, :]),
            'w_kv': bf(np.random.standard_normal((DI, DIM)) / np.sqrt(DIM) / s[None, :]),
            'sm_log': bf(np.linspace(3.0, 5.8, H) + 0.1 * np.random.standard_normal(H))}


def reference(tokens, w_qg, w_kv, sm_log):
    tq = mxq(f64(tokens), 2, 'e4m3')
    qg = (tq @ mxq(f64(w_qg), 1, 'e4m3').T).reshape(B, N, H, DK + DV).transpose(0, 2, 1, 3)
    kv = (tq @ mxq(f64(w_kv), 1, 'e4m3').T).reshape(B, N, H, DK + DV).transpose(0, 2, 1, 3)
    q, g = qg[..., :DK], qg[..., DK:]
    k, v = kv[..., :DK], kv[..., DK:]
    q, k, v = l2norm(q), l2norm(k), l2norm(v)
    w = np.exp(f64(sm_log)) + 1.0
    gamma = np.where(w < WT, 0.5 * (np.cos(np.pi * w / WT) + 1.0), 0.0)
    freq = np.pi * gamma / w
    ang = freq[:, None] * np.arange(N, dtype=np.float64)[None, :]
    cos = np.cos(ang)[None, :, :, None]
    sin = np.sin(ang)[None, :, :, None]

    def rotate(t):
        x0, x1 = t[..., 0:1], t[..., 1:2]
        return np.concatenate([x0 * cos - x1 * sin, x0 * sin + x1 * cos, t[..., 2:]], axis=-1)

    gate = np.tanh(g / (1.0 + np.exp(-g)))
    return rotate(q), gate, rotate(k), v

@@ -1,0 +1,349 @@
+import math
+from contextlib import ExitStack
+
+import concourse.mybir as mybir
+from concourse.masks import make_identity
+
+F32 = mybir.dt.float32
+BF16 = mybir.dt.bfloat16
+U32 = mybir.dt.uint32
+U8 = mybir.dt.uint8
+FP8X4 = mybir.dt.float8_e4m3fn_x4
+ACT = mybir.ActivationFunctionType
+ALU = mybir.AluOpType
+AXIS = mybir.AxisListType
+
+B, N, DIM, H, DK, DV = 8, 1024, 512, 2, 16, 48
+HEAD = DK + DV
+COLS = 2 * H * HEAD
+CHUNKS = 2 * H
+WT = 256.0
+EPS = 1e-12
+
+P = 128
+PACK = 4
+T = N // P
+HALF = T // 2
+HALVES = 2 * B
+BANKS = HALF // 2
+NARROW = HALF * CHUNKS
+WIDE = HALF * H
+
+ROUND_MAGIC = 1.5 * 2.0**23
+LOG_MAX = 6.0
+SUM_LAG = 2
+
+FLOPS = 2 * B * N * DIM * COLS
+
+
+def tile_gatedscreeningtile_pa_t_kernel(
+    tc, tokens, w_qg, w_kv, sm_log, out_0, out_1, out_2, out_3
+):
+    nc = tc.nc
+    with ExitStack() as ctx:
+        ctx.enter_context(tc.manual_schedule())
+        const = ctx.enter_context(tc.tile_pool(name="const", bufs=1))
+        resident = ctx.enter_context(tc.tile_pool(name="resident", bufs=1))
+        stage = ctx.enter_context(tc.tile_pool(name="stage", bufs=3))
+        squares = ctx.enter_context(tc.tile_pool(name="squares", bufs=SUM_LAG + 2))
+        results = ctx.enter_context(tc.tile_pool(name="results", bufs=4))
+
+        def live(h):
+            return 0 <= h < HALVES
+
+        def rows_of(dram, b):
+            return dram[b].rearrange("h (p t) d -> p h (t d)", t=T)
+
+        log_window = const.tile([P, H], BF16)
+        nc.scalar.dma_start(out=log_window[:], in_=sm_log.partition_broadcast(P))
+        w_rows = const.tile([P, 2, DIM], BF16)
+        nc.sync.dma_start(out=w_rows[:, 0, :], in_=w_qg)
+        nc.sync.dma_start(out=w_rows[:, 1, :], in_=w_kv)
+        x_rows = []
+        for h in range(HALVES):
+            x_h = resident.tile([P, HALF, DIM], BF16, name="x_rows%d" % h)
+            first = (h % 2) * HALF
+            nc.sync.dma_start(
+                out=x_h[:],
+                in_=tokens[h // 2].rearrange("(p t) k -> p t k", t=T)[:, first : first + HALF, :],
+            )
+            x_rows.append(x_h)
+
+        warm = const.tile([P, 1], F32)
+        nc.vector.memset(warm[:], 0.0)
+        nc.scalar.activation(out=warm[:], in_=warm[:], func=ACT.Silu)
+
+        ident = const.tile([P, P], F32)
+        make_identity(nc, ident[:])
+
+        two = const.tile([P, H], F32)
+        minus_one = const.tile([P, H], F32)
+        position = const.tile([P, T], F32)
+        window = const.tile([P, H], F32)
+        nc.gpsimd.memset(two[:], 2.0)
+        nc.gpsimd.memset(minus_one[:], -1.0)
+        nc.gpsimd.iota(
+            position[:], pattern=[[1, T]], base=0, channel_multiplier=T,
+            allow_small_or_imprecise_dtypes=True,
+        )
+        nc.gpsimd.tensor_scalar(
+            out=window[:], in0=log_window[:], scalar1=LOG_MAX, scalar2=1.0 / math.log(2.0),
+            op0=ALU.min, op1=ALU.mult,
+        )
+        nc.gpsimd.tensor_tensor(out=window[:], in0=two[:], in1=window[:], op=ALU.pow)
+        nc.gpsimd.tensor_scalar(
+            out=window[:], in0=window[:], scalar1=1.0, scalar2=WT, op0=ALU.add, op1=ALU.min
+        )
+        cos_window = const.tile([P, H], F32)
+        nc.scalar.activation(
+            out=cos_window[:], in_=window[:], func=ACT.Sin, scale=-math.pi / WT, bias=math.pi / 2
+        )
+        per_position = const.tile([P, H], F32)
+        nc.gpsimd.tensor_tensor(out=per_position[:], in0=window[:], in1=minus_one[:], op=ALU.pow)
+        nc.gpsimd.tensor_scalar_add(out=cos_window[:], in0=cos_window[:], scalar1=1.0)
+        nc.gpsimd.tensor_mul(out=per_position[:], in0=per_position[:], in1=cos_window[:])
+        turns = const.tile([P, H, T], F32)
+        for head in range(H):
+            nc.gpsimd.tensor_scalar(
+                out=turns[:, head, :], in0=position[:],
+                scalar1=per_position[:, head : head + 1], scalar2=0.25,
+                op0=ALU.mult, op1=ALU.mult,
+            )
+        whole = const.tile([P, H, T], F32)
+        nc.gpsimd.tensor_scalar(
+            out=whole[:], in0=turns[:], scalar1=ROUND_MAGIC, scalar2=ROUND_MAGIC,
+            op0=ALU.add, op1=ALU.subtract,
+        )
+        nc.gpsimd.tensor_sub(out=turns[:], in0=turns[:], in1=whole[:])
+
+        def finish_rotation_table():
+            sin_half = const.tile([P, H * T], F32)
+            sin_quarter = const.tile([P, H * T], F32)
+            flat_turns = turns[:].rearrange("p h t -> p (h t)")
+            nc.scalar.activation(out=sin_half[:], in_=flat_turns, func=ACT.Sin, scale=math.pi)
+            nc.scalar.activation(
+                out=sin_quarter[:], in_=flat_turns, func=ACT.Sin, scale=math.pi / 2
+            )
+            cos_half = const.tile([P, H * T], F32)
+            nc.gpsimd.tensor_mul(out=cos_half[:], in0=sin_quarter[:], in1=sin_quarter[:])
+            nc.gpsimd.tensor_scalar(
+                out=cos_half[:], in0=cos_half[:], scalar1=-2.0, scalar2=1.0,
+                op0=ALU.mult, op1=ALU.add,
+            )
+            half_sin_x = const.tile([P, H * T], F32)
+            nc.gpsimd.tensor_mul(out=half_sin_x[:], in0=sin_half[:], in1=cos_half[:])
+            sin_half_squared = const.tile([P, H * T], F32)
+            nc.gpsimd.tensor_mul(out=sin_half_squared[:], in0=sin_half[:], in1=sin_half[:])
+            table = const.tile([P, 2, H * T, 2, 2], F32, name="rotation")
+            for_q_and_k = [P, 2, H * T]
+            for diagonal in range(2):
+                nc.gpsimd.tensor_scalar(
+                    out=table[:, :, :, diagonal, diagonal],
+                    in0=sin_half_squared[:].unsqueeze(1).to_broadcast(for_q_and_k),
+                    scalar1=-2.0, scalar2=1.0, op0=ALU.mult, op1=ALU.add,
+                )
+            nc.gpsimd.tensor_scalar_mul(
+                out=table[:, :, :, 0, 1],
+                in0=half_sin_x[:].unsqueeze(1).to_broadcast(for_q_and_k), scalar1=-2.0,
+            )
+            nc.gpsimd.tensor_scalar_mul(
+                out=table[:, :, :, 1, 0],
+                in0=half_sin_x[:].unsqueeze(1).to_broadcast(for_q_and_k), scalar1=2.0,
+            )
+            return table
+
+        def flip(banks, rows, first):
+            words = rows[:].bitcast(F32)
+            flipped = banks.tile([P, 2, 2, P], F32, tag="flipped")
+            for j in range(2):
+                for u in range(2):
+                    nc.tensor.transpose(
+                        flipped[:, j, u, :], words[:, first + j, u : 2 * P : 2], ident[:]
+                    )
+            return flipped
+
+        def regroup(copy, flipped, grouped):
+            copy(
+                out=grouped.bitcast(F32).rearrange("p (j r u) -> p j r u", j=2, u=2),
+                in_=flipped[:].rearrange("p j u r -> p j r u"),
+            )
+
+        BANK_COLS = 2 * P * PACK
+        w_codes = const.tile([P, COLS], U32, align_bytes=64)
+        w_scales = const.tile([P, COLS], U8, align_bytes=64)
+        x_codes = []
+        x_scales = []
+        for h in range(HALVES):
+            x_codes.append(resident.tile([P, HALF * P], U32, name="x_codes%d" % h, align_bytes=64))
+            x_scales.append(resident.tile([P, HALF * P], U8, name="x_scales%d" % h, align_bytes=64))
+
+        def project(banks, h):
+            products = []
+            for i in range(BANKS):
+                acc = banks.tile([P, 2, COLS], F32, tag="acc")
+                for j in range(2):
+                    cols = slice((2 * i + j) * P, (2 * i + j + 1) * P)
+                    nc.tensor.matmul_mx(
+                        out=acc[:, j, :],
+                        lhsT=x_codes[h][:, cols].bitcast(FP8X4),
+                        lhsT_scale=x_scales[h][:, cols],
+                        rhs=w_codes[:].bitcast(FP8X4),
+                        rhs_scale=w_scales[:],
+                        start=True,
+                        stop=True,
+                    )
+                products.append(acc[:].rearrange("p j (c d) -> p j c d", d=HEAD))
+            return products
+
+        sum_squares = const.tile([P, HALVES, NARROW + WIDE], F32)
+        flipped_of = {}
+        grouped_of = {}
+        acc_of = {}
+        squares_of = {}
+        gate_of = {}
+
+        with tc.psum_pool(name="flip_banks", bufs=4) as flip_banks, tc.psum_pool(
+            name="acc_banks", bufs=4
+        ) as acc_banks:
+            w_grouped = const.tile([P, BANK_COLS], BF16, align_bytes=64)
+            regroup(nc.vector.tensor_copy, flip(flip_banks, w_rows, 0), w_grouped[:])
+            nc.vector.quantize_mx(
+                out=w_codes[:].bitcast(FP8X4), scales=w_scales[:], in_=w_grouped[:]
+            )
+
+            def first_sweep_step(h):
+                if live(h + 3):
+                    flipped_of[h + 3] = [
+                        flip(flip_banks, x_rows[h + 3], 2 * i) for i in range(BANKS)
+                    ]
+                if live(h + 1):
+                    nc.vector.quantize_mx(
+                        out=x_codes[h + 1][:].bitcast(FP8X4), scales=x_scales[h + 1][:],
+                        in_=grouped_of[h + 1][:],
+                    )
+                    acc_of[h + 1] = project(acc_banks, h + 1)
+                if live(h - SUM_LAG - 1):
+                    nc.vector.tensor_scalar_max(
+                        out=sum_squares[:, h - SUM_LAG - 1, :],
+                        in0=sum_squares[:, h - SUM_LAG - 1, :], scalar1=EPS * EPS,
+                    )
+                if live(h):
+                    if h % 2 == 0:
+                        gate_of[h // 2] = results.tile([P, H, T, DV], F32, name="gate", tag="gate")
+                    gate = gate_of[h // 2]
+                    sq_narrow = squares.tile([P, HALF, CHUNKS, DK], F32, tag="sq_narrow")
+                    sq_wide = squares.tile([P, HALF, H, DV], F32, tag="sq_wide")
+                    squares_of[h] = (sq_narrow, sq_wide)
+                    for i in range(BANKS):
+                        acc = acc_of[h][i]
+                        here = slice(2 * i, 2 * i + 2)
+                        there = slice((h % 2) * HALF + 2 * i, (h % 2) * HALF + 2 * i + 2)
+                        nc.scalar.activation(
+                            out=sq_narrow[:, here, :, :], in_=acc[:, :, :, 0:DK], func=ACT.Square
+                        )
+                        nc.scalar.activation(
+                            out=sq_wide[:, here, :, :], in_=acc[:, :, H:CHUNKS, DK:HEAD],
+                            func=ACT.Square,
+                        )
+                        nc.scalar.activation(
+                            out=gate[:, :, there, :].rearrange("p h j d -> p j h d"),
+                            in_=acc[:, :, 0:H, DK:HEAD], func=ACT.Silu,
+                        )
+                if live(h + 2):
+                    grouped = stage.tile([P, BANKS * BANK_COLS], BF16, tag="grouped", align_bytes=64)
+                    grouped_of[h + 2] = grouped
+                    first_copy = nc.scalar.copy if h % 2 == 0 else nc.vector.tensor_copy
+                    regroup(first_copy, flipped_of[h + 2][0], grouped[:, 0:BANK_COLS])
+                    regroup(nc.vector.tensor_copy, flipped_of[h + 2][1], grouped[:, BANK_COLS:])
+                if live(h - SUM_LAG):
+                    sq_narrow, sq_wide = squares_of[h - SUM_LAG]
+                    nc.vector.tensor_reduce(
+                        out=sum_squares[:, h - SUM_LAG, 0:NARROW],
+                        in_=sq_narrow[:].rearrange("p t c d -> p (t c) d"), axis=AXIS.X, op=ALU.add,
+                    )
+                    nc.vector.tensor_reduce(
+                        out=sum_squares[:, h - SUM_LAG, NARROW:],
+                        in_=sq_wide[:].rearrange("p t h d -> p (t h) d"), axis=AXIS.X, op=ALU.add,
+                    )
+                if live(h - 1):
+                    gate = gate_of[(h - 1) // 2]
+                    there = slice(((h - 1) % 2) * HALF, ((h - 1) % 2 + 1) * HALF)
+                    nc.scalar.activation(
+                        out=gate[:, :, there, :], in_=gate[:, :, there, :], func=ACT.Tanh
+                    )
+                    if (h - 1) % 2 == 1:
+                        nc.sync.dma_start(
+                            out=rows_of(out_1, (h - 1) // 2),
+                            in_=gate[:].rearrange("p h t d -> p h (t d)"),
+                        )
+
+            for h in range(-3, HALVES // 2):
+                first_sweep_step(h)
+            rotation = finish_rotation_table()
+            for h in range(HALVES // 2, HALVES + SUM_LAG + 2):
+                first_sweep_step(h)
+
+        inverse_norm = const.tile([P, HALVES, NARROW + WIDE], F32)
+        for part in (slice(0, HALVES // 2), slice(HALVES // 2, HALVES)):
+            nc.scalar.activation(
+                out=inverse_norm[:, part, :], in_=sum_squares[:, part, :],
+                func=ACT.Abs_reciprocal_sqrt,
+            )
+
+        again_banks = ctx.enter_context(tc.psum_pool(name="again_banks", bufs=8))
+        AHEAD = 2
+        for h in range(AHEAD):
+            acc_of[h] = project(again_banks, h)
+        for h in range(HALVES):
+            b = h // 2
+            if live(h + AHEAD):
+                acc_of[h + AHEAD] = project(again_banks, h + AHEAD)
+            if h % 2 == 0:
+                qk = results.tile([P, CHUNKS, T, DK], F32, tag="qk")
+                v_n = results.tile([P, H, T, DV], F32, tag="v_n")
+            for i in range(BANKS):
+                there = slice((h % 2) * HALF + 2 * i, (h % 2) * HALF + 2 * i + 2)
+                narrow = inverse_norm[:, h, 2 * i * CHUNKS : (2 * i + 2) * CHUNKS]
+                nc.vector.tensor_tensor(
+                    out=qk[:, :, there, :].rearrange("p c j d -> p j c d"),
+                    in0=acc_of[h][i][:, :, :, 0:DK],
+                    in1=narrow.rearrange("p (j c) -> p j c", j=2)
+                    .unsqueeze(3)
+                    .to_broadcast([P, 2, CHUNKS, DK]),
+                    op=ALU.mult,
+                )
+            if h % 2 == 1:
+                pair = qk[:].rearrange("p c t d -> p (c t) d")[:, :, 0:2]
+                products = stage.tile([P, CHUNKS * T, 2, 2], F32, tag="products")
+                nc.gpsimd.tensor_tensor(
+                    out=products[:],
+                    in0=pair.unsqueeze(2).to_broadcast([P, CHUNKS * T, 2, 2]),
+                    in1=rotation[:].rearrange("p w g r c -> p (w g) r c"),
+                    op=ALU.mult,
+                )
+                nc.gpsimd.tensor_add(
+                    out=pair, in0=products[:, :, :, 0], in1=products[:, :, :, 1]
+                )
+            for i in range(BANKS):
+                there = slice((h % 2) * HALF + 2 * i, (h % 2) * HALF + 2 * i + 2)
+                wide = inverse_norm[:, h, NARROW + 2 * i * H : NARROW + (2 * i + 2) * H]
+                nc.vector.tensor_tensor(
+                    out=v_n[:, :, there, :].rearrange("p h j d -> p j h d"),
+                    in0=acc_of[h][i][:, :, H:CHUNKS, DK:HEAD],
+                    in1=wide.rearrange("p (j h) -> p j h", j=2)
+                    .unsqueeze(3)
+                    .to_broadcast([P, 2, H, DV]),
+                    op=ALU.mult,
+                )
+            if h % 2 == 1:
+                nc.sync.dma_start(
+                    out=rows_of(out_3, b), in_=v_n[:].rearrange("p h t d -> p h (t d)")
+                )
+                nc.sync.dma_start(
+                    out=rows_of(out_0, b),
+                    in_=qk[:, 0:H, :, :].rearrange("p h t d -> p h (t d)"),
+                )
+                nc.sync.dma_start(
+                    out=rows_of(out_2, b),
+                    in_=qk[:, H:CHUNKS, :, :].rearrange("p h t d -> p h (t d)"),
+                )

@@ -26,12 +26,27 @@ T = N // P
 HALF = T // 2
 HALVES = 2 * B
 BANKS = HALF // 2
-NARROW = HALF * CHUNKS
-WIDE = HALF * H
+NARROW = T * CHUNKS
+WIDE = T * H
+QK = CHUNKS * DK
+QKV = QK + H * DV
 
 ROUND_MAGIC = 1.5 * 2.0**23
 LOG_MAX = 6.0
-SUM_LAG = 2
+
+FOLDS = 2
+SHARE = True
+SUM_LAG = 3
+SUMMED = 7
+SPLIT = 4
+SPLIT_AT = 6
+
+
+def by_vector(h, i):
+    return VPAT[h] > i
+
+
+VPAT = [1, 2] * 8
 
 FLOPS = 2 * B * N * DIM * COLS
 
@@ -45,7 +60,6 @@ def tile_gatedscreeningtile_pa_t_kernel(
         const = ctx.enter_context(tc.tile_pool(name="const", bufs=1))
         resident = ctx.enter_context(tc.tile_pool(name="resident", bufs=1))
         stage = ctx.enter_context(tc.tile_pool(name="stage", bufs=3))
-        squares = ctx.enter_context(tc.tile_pool(name="squares", bufs=SUM_LAG + 2))
         results = ctx.enter_context(tc.tile_pool(name="results", bufs=4))
 
         def live(h):
@@ -152,10 +166,10 @@ def tile_gatedscreeningtile_pa_t_kernel(
             )
             return table
 
-        def flip(banks, rows, first):
+        def flip(banks, rows, first, count):
             words = rows[:].bitcast(F32)
             flipped = banks.tile([P, 2, 2, P], F32, tag="flipped")
-            for j in range(2):
+            for j in range(count):
                 for u in range(2):
                     nc.tensor.transpose(
                         flipped[:, j, u, :], words[:, first + j, u : 2 * P : 2], ident[:]
@@ -192,21 +206,72 @@ def tile_gatedscreeningtile_pa_t_kernel(
                         start=True,
                         stop=True,
                     )
-                products.append(acc[:].rearrange("p j (c d) -> p j c d", d=HEAD))
+                products.append(acc)
             return products
 
-        sum_squares = const.tile([P, HALVES, NARROW + WIDE], F32)
+        sums = const.tile([P, B, NARROW + WIDE], F32)
+        inverse = const.tile([P, B, NARROW + WIDE], F32)
         flipped_of = {}
         grouped_of = {}
         acc_of = {}
         squares_of = {}
+        folded_of = {}
         gate_of = {}
+
+        def fold(b):
+            sq = squares_of[b]
+            q = sq[:, :, 0:QK].rearrange("p t (c d) -> p t c d", d=DK)
+            v = sq[:, :, QK:].rearrange("p t (h d) -> p t h d", h=H)
+            for level in range(FOLDS):
+                dk = DK // 2 ** (level + 1)
+                dv = DV // 2 ** (level + 1)
+                less_v = stage.tile([P, T, H, dv], F32, name="less_v%d" % level, tag="less_v%d" % level)
+                less_q = stage.tile([P, T, CHUNKS, dk], F32, name="less_q%d" % level, tag="less_q%d" % level)
+                nc.gpsimd.tensor_add(out=less_v[:], in0=v[:, :, :, 0:dv], in1=v[:, :, :, dv : 2 * dv])
+                nc.gpsimd.tensor_add(out=less_q[:], in0=q[:, :, :, 0:dk], in1=q[:, :, :, dk : 2 * dk])
+                v = less_v[:]
+                q = less_q[:]
+            folded_of[b] = (q, v)
+
+        def reduce(b):
+            q, v = folded_of[b]
+            nc.vector.tensor_reduce(
+                out=sums[:, b, 0:NARROW].rearrange("p (t c) -> p t c", t=T), in_=q,
+                axis=AXIS.X, op=ALU.add,
+            )
+            nc.vector.tensor_reduce(
+                out=sums[:, b, NARROW:].rearrange("p (t h) -> p t h", t=T), in_=v,
+                axis=AXIS.X, op=ALU.add,
+            )
+
+        def invert(lo, hi):
+            nc.vector.tensor_scalar_max(
+                out=sums[:, lo:hi, :], in0=sums[:, lo:hi, :], scalar1=EPS * EPS
+            )
+            nc.scalar.activation(
+                out=inverse[:, lo:hi, :], in_=sums[:, lo:hi, :], func=ACT.Abs_reciprocal_sqrt
+            )
 
         with tc.psum_pool(name="flip_banks", bufs=4) as flip_banks, tc.psum_pool(
             name="acc_banks", bufs=4
         ) as acc_banks:
-            w_grouped = const.tile([P, BANK_COLS], BF16, align_bytes=64)
-            regroup(nc.vector.tensor_copy, flip(flip_banks, w_rows, 0), w_grouped[:])
+            w_grouped = const.tile([P, COLS * PACK], BF16, align_bytes=64)
+            w_words = w_grouped[:].bitcast(F32).rearrange("p (n u) -> p n u", u=2)
+
+            def place(copy, flipped, lo, hi, first):
+                copy(
+                    out=w_words[:, first : first + H * (hi - lo), :].rearrange(
+                        "p (h d) u -> p h d u", h=H
+                    ),
+                    in_=flipped[:, 0, :, :].rearrange("p u (h d) -> p h d u", h=H)[:, :, lo:hi, :],
+                )
+
+            qg_flipped = flip(flip_banks, w_rows, 0, 1)
+            kv_flipped = flip(flip_banks, w_rows, 1, 1)
+            place(nc.vector.tensor_copy, qg_flipped, 0, DK, 0)
+            place(nc.scalar.copy, kv_flipped, 0, DK, H * DK)
+            place(nc.scalar.copy, kv_flipped, DK, HEAD, QK)
+            place(nc.vector.tensor_copy, qg_flipped, DK, HEAD, QKV)
             nc.vector.quantize_mx(
                 out=w_codes[:].bitcast(FP8X4), scales=w_scales[:], in_=w_grouped[:]
             )
@@ -214,7 +279,7 @@ def tile_gatedscreeningtile_pa_t_kernel(
             def first_sweep_step(h):
                 if live(h + 3):
                     flipped_of[h + 3] = [
-                        flip(flip_banks, x_rows[h + 3], 2 * i) for i in range(BANKS)
+                        flip(flip_banks, x_rows[h + 3], 2 * i, 2) for i in range(BANKS)
                     ]
                 if live(h + 1):
                     nc.vector.quantize_mx(
@@ -222,49 +287,35 @@ def tile_gatedscreeningtile_pa_t_kernel(
                         in_=grouped_of[h + 1][:],
                     )
                     acc_of[h + 1] = project(acc_banks, h + 1)
-                if live(h - SUM_LAG - 1):
-                    nc.vector.tensor_scalar_max(
-                        out=sum_squares[:, h - SUM_LAG - 1, :],
-                        in0=sum_squares[:, h - SUM_LAG - 1, :], scalar1=EPS * EPS,
-                    )
-                if live(h):
-                    if h % 2 == 0:
-                        gate_of[h // 2] = results.tile([P, H, T, DV], F32, name="gate", tag="gate")
-                    gate = gate_of[h // 2]
-                    sq_narrow = squares.tile([P, HALF, CHUNKS, DK], F32, tag="sq_narrow")
-                    sq_wide = squares.tile([P, HALF, H, DV], F32, tag="sq_wide")
-                    squares_of[h] = (sq_narrow, sq_wide)
-                    for i in range(BANKS):
-                        acc = acc_of[h][i]
-                        here = slice(2 * i, 2 * i + 2)
-                        there = slice((h % 2) * HALF + 2 * i, (h % 2) * HALF + 2 * i + 2)
-                        nc.scalar.activation(
-                            out=sq_narrow[:, here, :, :], in_=acc[:, :, :, 0:DK], func=ACT.Square
-                        )
-                        nc.scalar.activation(
-                            out=sq_wide[:, here, :, :], in_=acc[:, :, H:CHUNKS, DK:HEAD],
-                            func=ACT.Square,
-                        )
-                        nc.scalar.activation(
-                            out=gate[:, :, there, :].rearrange("p h j d -> p j h d"),
-                            in_=acc[:, :, 0:H, DK:HEAD], func=ACT.Silu,
-                        )
                 if live(h + 2):
                     grouped = stage.tile([P, BANKS * BANK_COLS], BF16, tag="grouped", align_bytes=64)
                     grouped_of[h + 2] = grouped
-                    first_copy = nc.scalar.copy if h % 2 == 0 else nc.vector.tensor_copy
-                    regroup(first_copy, flipped_of[h + 2][0], grouped[:, 0:BANK_COLS])
-                    regroup(nc.vector.tensor_copy, flipped_of[h + 2][1], grouped[:, BANK_COLS:])
-                if live(h - SUM_LAG):
-                    sq_narrow, sq_wide = squares_of[h - SUM_LAG]
-                    nc.vector.tensor_reduce(
-                        out=sum_squares[:, h - SUM_LAG, 0:NARROW],
-                        in_=sq_narrow[:].rearrange("p t c d -> p (t c) d"), axis=AXIS.X, op=ALU.add,
-                    )
-                    nc.vector.tensor_reduce(
-                        out=sum_squares[:, h - SUM_LAG, NARROW:],
-                        in_=sq_wide[:].rearrange("p t h d -> p (t h) d"), axis=AXIS.X, op=ALU.add,
-                    )
+                    for i in range(BANKS):
+                        copy = nc.vector.tensor_copy if by_vector(h + 2, i) else nc.scalar.copy
+                        regroup(
+                            copy, flipped_of[h + 2][i],
+                            grouped[:, i * BANK_COLS : (i + 1) * BANK_COLS],
+                        )
+                if live(h):
+                    if h % 2 == 0:
+                        gate_of[h // 2] = results.tile([P, H, T, DV], F32, name="gate", tag="gate")
+                        squares_of[h // 2] = stage.tile([P, T, QKV], F32, name="sq", tag="sq")
+                    for i in range(BANKS):
+                        acc = acc_of[h][i]
+                        there = slice((h % 2) * HALF + 2 * i, (h % 2) * HALF + 2 * i + 2)
+                        nc.scalar.activation(
+                            out=squares_of[h // 2][:, there, :], in_=acc[:, :, 0:QKV],
+                            func=ACT.Square,
+                        )
+                        nc.scalar.activation(
+                            out=gate_of[h // 2][:, :, there, :].rearrange("p h j d -> p j h d"),
+                            in_=acc[:, :, QKV:].rearrange("p j (h d) -> p j h d", h=H),
+                            func=ACT.Silu,
+                        )
+                    if h % 2 == 1:
+                        fold(h // 2)
+                if h % 2 == 1 and live(h - SUM_LAG):
+                    reduce((h - SUM_LAG) // 2)
                 if live(h - 1):
                     gate = gate_of[(h - 1) // 2]
                     there = slice(((h - 1) % 2) * HALF, ((h - 1) % 2 + 1) * HALF)
@@ -280,36 +331,36 @@ def tile_gatedscreeningtile_pa_t_kernel(
             for h in range(-3, HALVES // 2):
                 first_sweep_step(h)
             rotation = finish_rotation_table()
-            for h in range(HALVES // 2, HALVES + SUM_LAG + 2):
+            for h in range(HALVES // 2, HALVES + 1):
                 first_sweep_step(h)
 
-        inverse_norm = const.tile([P, HALVES, NARROW + WIDE], F32)
-        for part in (slice(0, HALVES // 2), slice(HALVES // 2, HALVES)):
-            nc.scalar.activation(
-                out=inverse_norm[:, part, :], in_=sum_squares[:, part, :],
-                func=ACT.Abs_reciprocal_sqrt,
-            )
-
         again_banks = ctx.enter_context(tc.psum_pool(name="again_banks", bufs=8))
+        for b in range(SUMMED, SPLIT):
+            reduce(b)
+        invert(0, SPLIT)
+
         AHEAD = 2
         for h in range(AHEAD):
             acc_of[h] = project(again_banks, h)
         for h in range(HALVES):
             b = h // 2
+            if h == SPLIT_AT:
+                for k in range(max(SPLIT, SUMMED), B):
+                    reduce(k)
+                invert(SPLIT, B)
             if live(h + AHEAD):
                 acc_of[h + AHEAD] = project(again_banks, h + AHEAD)
             if h % 2 == 0:
                 qk = results.tile([P, CHUNKS, T, DK], F32, tag="qk")
                 v_n = results.tile([P, H, T, DV], F32, tag="v_n")
+            narrow = inverse[:, b, 0:NARROW].rearrange("p (t c) -> p t c", t=T)
+            wide = inverse[:, b, NARROW:].rearrange("p (t h) -> p t h", t=T)
             for i in range(BANKS):
                 there = slice((h % 2) * HALF + 2 * i, (h % 2) * HALF + 2 * i + 2)
-                narrow = inverse_norm[:, h, 2 * i * CHUNKS : (2 * i + 2) * CHUNKS]
                 nc.vector.tensor_tensor(
                     out=qk[:, :, there, :].rearrange("p c j d -> p j c d"),
-                    in0=acc_of[h][i][:, :, :, 0:DK],
-                    in1=narrow.rearrange("p (j c) -> p j c", j=2)
-                    .unsqueeze(3)
-                    .to_broadcast([P, 2, CHUNKS, DK]),
+                    in0=acc_of[h][i][:, :, 0:QK].rearrange("p j (c d) -> p j c d", d=DK),
+                    in1=narrow[:, there, :].unsqueeze(3).to_broadcast([P, 2, CHUNKS, DK]),
                     op=ALU.mult,
                 )
             if h % 2 == 1:
@@ -326,13 +377,21 @@ def tile_gatedscreeningtile_pa_t_kernel(
                 )
             for i in range(BANKS):
                 there = slice((h % 2) * HALF + 2 * i, (h % 2) * HALF + 2 * i + 2)
-                wide = inverse_norm[:, h, NARROW + 2 * i * H : NARROW + (2 * i + 2) * H]
+                if i == 1 and SHARE:
+                    for j in range(2):
+                        for head in range(H):
+                            t = there.start + j
+                            nc.scalar.activation(
+                                out=v_n[:, head, t, :],
+                                in_=acc_of[h][i][:, j, QK + head * DV : QK + (head + 1) * DV],
+                                func=ACT.Copy,
+                                scale=wide[:, t, head : head + 1],
+                            )
+                    continue
                 nc.vector.tensor_tensor(
                     out=v_n[:, :, there, :].rearrange("p h j d -> p j h d"),
-                    in0=acc_of[h][i][:, :, H:CHUNKS, DK:HEAD],
-                    in1=wide.rearrange("p (j h) -> p j h", j=2)
-                    .unsqueeze(3)
-                    .to_broadcast([P, 2, H, DV]),
+                    in0=acc_of[h][i][:, :, QK:QKV].rearrange("p j (h d) -> p j h d", h=H),
+                    in1=wide[:, there, :].unsqueeze(3).to_broadcast([P, 2, H, DV]),
                     op=ALU.mult,
                 )
             if h % 2 == 1:

@@ -34,7 +34,7 @@ QKV = QK + H * DV
 ROUND_MAGIC = 1.5 * 2.0**23
 LOG_MAX = 6.0
 
-FOLDS = 2
+FOLDS = 0
 SHARE = True
 SUM_LAG = 3
 SUMMED = 7

@@ -19,6 +19,7 @@ COLS = 2 * H * HEAD
 CHUNKS = 2 * H
 WT = 256.0
 EPS = 1e-12
+RSQRT_MAGIC = float(0x5F3759DF)
 
 P = 128
 PACK = 4
@@ -35,18 +36,21 @@ ROUND_MAGIC = 1.5 * 2.0**23
 LOG_MAX = 6.0
 
 FOLDS = 0
-SHARE = True
+EARLY = 2
+TURNS_AT = 1
+MMFIRST = -9
+NEWTON_AT = 6
+SHARE = 4
+LASTSUM = 3
 SUM_LAG = 3
 SUMMED = 7
-SPLIT = 4
-SPLIT_AT = 6
 
 
 def by_vector(h, i):
     return VPAT[h] > i
 
 
-VPAT = [1, 2] * 8
+VPAT = [1, 1, 1, 2] * 4
 
 FLOPS = 2 * B * N * DIM * COLS
 
@@ -60,7 +64,8 @@ def tile_gatedscreeningtile_pa_t_kernel(
         const = ctx.enter_context(tc.tile_pool(name="const", bufs=1))
         resident = ctx.enter_context(tc.tile_pool(name="resident", bufs=1))
         stage = ctx.enter_context(tc.tile_pool(name="stage", bufs=3))
-        results = ctx.enter_context(tc.tile_pool(name="results", bufs=4))
+        results = ctx.enter_context(tc.tile_pool(name="results", bufs=8))
+        deep = ctx.enter_context(tc.tile_pool(name="deep", bufs=4))
 
         def live(h):
             return 0 <= h < HALVES
@@ -77,10 +82,9 @@ def tile_gatedscreeningtile_pa_t_kernel(
         for h in range(HALVES):
             x_h = resident.tile([P, HALF, DIM], BF16, name="x_rows%d" % h)
             first = (h % 2) * HALF
-            nc.sync.dma_start(
-                out=x_h[:],
-                in_=tokens[h // 2].rearrange("(p t) k -> p t k", t=T)[:, first : first + HALF, :],
-            )
+            rows = tokens[h // 2].rearrange("(p t) k -> p t k", t=T)[:, first : first + HALF, :]
+            for part in (slice(0, 2), slice(2, 4)) if h == 0 else (slice(0, HALF),):
+                nc.sync.dma_start(out=x_h[:, part, :], in_=rows[:, part, :])
             x_rows.append(x_h)
 
         warm = const.tile([P, 1], F32)
@@ -109,26 +113,28 @@ def tile_gatedscreeningtile_pa_t_kernel(
             out=window[:], in0=window[:], scalar1=1.0, scalar2=WT, op0=ALU.add, op1=ALU.min
         )
         cos_window = const.tile([P, H], F32)
-        nc.scalar.activation(
-            out=cos_window[:], in_=window[:], func=ACT.Sin, scale=-math.pi / WT, bias=math.pi / 2
-        )
         per_position = const.tile([P, H], F32)
-        nc.gpsimd.tensor_tensor(out=per_position[:], in0=window[:], in1=minus_one[:], op=ALU.pow)
-        nc.gpsimd.tensor_scalar_add(out=cos_window[:], in0=cos_window[:], scalar1=1.0)
-        nc.gpsimd.tensor_mul(out=per_position[:], in0=per_position[:], in1=cos_window[:])
         turns = const.tile([P, H, T], F32)
-        for head in range(H):
-            nc.gpsimd.tensor_scalar(
-                out=turns[:, head, :], in0=position[:],
-                scalar1=per_position[:, head : head + 1], scalar2=0.25,
-                op0=ALU.mult, op1=ALU.mult,
-            )
         whole = const.tile([P, H, T], F32)
-        nc.gpsimd.tensor_scalar(
-            out=whole[:], in0=turns[:], scalar1=ROUND_MAGIC, scalar2=ROUND_MAGIC,
-            op0=ALU.add, op1=ALU.subtract,
-        )
-        nc.gpsimd.tensor_sub(out=turns[:], in0=turns[:], in1=whole[:])
+
+        def find_turns():
+            nc.scalar.activation(
+                out=cos_window[:], in_=window[:], func=ACT.Sin, scale=-math.pi / WT, bias=math.pi / 2
+            )
+            nc.gpsimd.tensor_tensor(out=per_position[:], in0=window[:], in1=minus_one[:], op=ALU.pow)
+            nc.gpsimd.tensor_scalar_add(out=cos_window[:], in0=cos_window[:], scalar1=1.0)
+            nc.gpsimd.tensor_mul(out=per_position[:], in0=per_position[:], in1=cos_window[:])
+            for head in range(H):
+                nc.gpsimd.tensor_scalar(
+                    out=turns[:, head, :], in0=position[:],
+                    scalar1=per_position[:, head : head + 1], scalar2=0.25,
+                    op0=ALU.mult, op1=ALU.mult,
+                )
+            nc.gpsimd.tensor_scalar(
+                out=whole[:], in0=turns[:], scalar1=ROUND_MAGIC, scalar2=ROUND_MAGIC,
+                op0=ALU.add, op1=ALU.subtract,
+            )
+            nc.gpsimd.tensor_sub(out=turns[:], in0=turns[:], in1=whole[:])
 
         def finish_rotation_table():
             sin_half = const.tile([P, H * T], F32)
@@ -244,13 +250,37 @@ def tile_gatedscreeningtile_pa_t_kernel(
                 axis=AXIS.X, op=ALU.add,
             )
 
-        def invert(lo, hi):
+        def clamp(lo, hi):
             nc.vector.tensor_scalar_max(
                 out=sums[:, lo:hi, :], in0=sums[:, lo:hi, :], scalar1=EPS * EPS
             )
+
+        def invert(lo, hi):
             nc.scalar.activation(
                 out=inverse[:, lo:hi, :], in_=sums[:, lo:hi, :], func=ACT.Abs_reciprocal_sqrt
             )
+
+        def newton(lo, hi):
+            shape = [P, hi - lo, NARROW + WIDE]
+            s = sums[:, lo:hi, :]
+            guess = const.tile(shape, U32, name="guess%d" % lo)
+            y = const.tile(shape, F32, name="y0_%d" % lo)
+            nc.scalar.activation(
+                out=guess[:], in_=s.bitcast(U32), func=ACT.Identity, scale=-0.5, bias=RSQRT_MAGIC
+            )
+            nc.scalar.copy(out=y[:], in_=guess[:].bitcast(F32))
+            y = y[:]
+            for k in range(4):
+                t = const.tile(shape, F32, name="t%d_%d" % (k, lo))
+                better = const.tile(shape, F32, name="y%d_%d" % (k + 1, lo))
+                out = inverse[:, lo:hi, :] if k == 3 else better[:]
+                nc.gpsimd.tensor_mul(out=t[:], in0=y, in1=y)
+                nc.gpsimd.tensor_mul(out=t[:], in0=t[:], in1=s)
+                nc.gpsimd.tensor_scalar(
+                    out=t[:], in0=t[:], scalar1=-0.5, scalar2=1.5, op0=ALU.mult, op1=ALU.add
+                )
+                nc.gpsimd.tensor_mul(out=out, in0=y, in1=t[:])
+                y = out
 
         with tc.psum_pool(name="flip_banks", bufs=4) as flip_banks, tc.psum_pool(
             name="acc_banks", bufs=4
@@ -277,23 +307,29 @@ def tile_gatedscreeningtile_pa_t_kernel(
             )
 
             def first_sweep_step(h):
-                if live(h + 3):
-                    flipped_of[h + 3] = [
-                        flip(flip_banks, x_rows[h + 3], 2 * i, 2) for i in range(BANKS)
-                    ]
+                def flip_ahead():
+                    if live(h + 4):
+                        flipped_of[h + 4] = [
+                            flip(flip_banks, x_rows[h + 4], 2 * i, 2) for i in range(BANKS)
+                        ]
+
+                if h >= MMFIRST:
+                    flip_ahead()
                 if live(h + 1):
                     nc.vector.quantize_mx(
                         out=x_codes[h + 1][:].bitcast(FP8X4), scales=x_scales[h + 1][:],
                         in_=grouped_of[h + 1][:],
                     )
                     acc_of[h + 1] = project(acc_banks, h + 1)
-                if live(h + 2):
-                    grouped = stage.tile([P, BANKS * BANK_COLS], BF16, tag="grouped", align_bytes=64)
-                    grouped_of[h + 2] = grouped
+                if h < MMFIRST:
+                    flip_ahead()
+                if live(h + 3):
+                    grouped = deep.tile([P, BANKS * BANK_COLS], BF16, tag="grouped", align_bytes=64)
+                    grouped_of[h + 3] = grouped
                     for i in range(BANKS):
-                        copy = nc.vector.tensor_copy if by_vector(h + 2, i) else nc.scalar.copy
+                        copy = nc.vector.tensor_copy if by_vector(h + 3, i) else nc.scalar.copy
                         regroup(
-                            copy, flipped_of[h + 2][i],
+                            copy, flipped_of[h + 3][i],
                             grouped[:, i * BANK_COLS : (i + 1) * BANK_COLS],
                         )
                 if live(h):
@@ -316,6 +352,11 @@ def tile_gatedscreeningtile_pa_t_kernel(
                         fold(h // 2)
                 if h % 2 == 1 and live(h - SUM_LAG):
                     reduce((h - SUM_LAG) // 2)
+                for k in range(EARLY // 2):
+                    if h == NEWTON_AT + 4 * k:
+                        clamp(2 * k, 2 * k + 2)
+                    if h == NEWTON_AT + 4 * k + 1:
+                        newton(2 * k, 2 * k + 2)
                 if live(h - 1):
                     gate = gate_of[(h - 1) // 2]
                     there = slice(((h - 1) % 2) * HALF, ((h - 1) % 2 + 1) * HALF)
@@ -328,26 +369,25 @@ def tile_gatedscreeningtile_pa_t_kernel(
                             in_=gate[:].rearrange("p h t d -> p h (t d)"),
                         )
 
-            for h in range(-3, HALVES // 2):
+            for h in range(-4, HALVES // 2):
+                if h == TURNS_AT:
+                    find_turns()
                 first_sweep_step(h)
             rotation = finish_rotation_table()
             for h in range(HALVES // 2, HALVES + 1):
                 first_sweep_step(h)
 
         again_banks = ctx.enter_context(tc.psum_pool(name="again_banks", bufs=8))
-        for b in range(SUMMED, SPLIT):
-            reduce(b)
-        invert(0, SPLIT)
-
         AHEAD = 2
         for h in range(AHEAD):
             acc_of[h] = project(again_banks, h)
         for h in range(HALVES):
             b = h // 2
-            if h == SPLIT_AT:
-                for k in range(max(SPLIT, SUMMED), B):
+            if h == LASTSUM:
+                for k in range(SUMMED, B):
                     reduce(k)
-                invert(SPLIT, B)
+                clamp(EARLY, B)
+                invert(EARLY, B)
             if live(h + AHEAD):
                 acc_of[h + AHEAD] = project(again_banks, h + AHEAD)
             if h % 2 == 0:
@@ -377,7 +417,7 @@ def tile_gatedscreeningtile_pa_t_kernel(
                 )
             for i in range(BANKS):
                 there = slice((h % 2) * HALF + 2 * i, (h % 2) * HALF + 2 * i + 2)
-                if i == 1 and SHARE:
+                if i == 1 and h >= SHARE:
                     for j in range(2):
                         for head in range(H):
                             t = there.start + j

@@ -37,6 +37,10 @@ LOG_MAX = 6.0
 
 FOLDS = 0
 EARLY = 2
+GPOS = 1
+TABLE_AT = 8
+ONLY = 4
+LATE = {15: [0], 16: [1]}
 TURNS_AT = 1
 MMFIRST = -9
 NEWTON_AT = 6
@@ -50,7 +54,7 @@ def by_vector(h, i):
     return VPAT[h] > i
 
 
-VPAT = [1, 1, 1, 2] * 4
+VPAT = [1, 1, 1, 2] + [1, 2, 1, 1] * 2 + [1, 1, 2, 2]
 
 FLOPS = 2 * B * N * DIM * COLS
 
@@ -282,9 +286,77 @@ def tile_gatedscreeningtile_pa_t_kernel(
                 nc.gpsimd.tensor_mul(out=out, in0=y, in1=t[:])
                 y = out
 
-        with tc.psum_pool(name="flip_banks", bufs=4) as flip_banks, tc.psum_pool(
-            name="acc_banks", bufs=4
-        ) as acc_banks:
+        out_of = {}
+
+        def scale(h):
+            b = h // 2
+            if h % 2 == 0:
+                out_of[b] = (
+                    results.tile([P, CHUNKS, T, DK], F32, name="qk", tag="qk"),
+                    results.tile([P, H, T, DV], F32, name="v_n", tag="v_n"),
+                )
+            qk, v_n = out_of[b]
+            narrow = inverse[:, b, 0:NARROW].rearrange("p (t c) -> p t c", t=T)
+            wide = inverse[:, b, NARROW:].rearrange("p (t h) -> p t h", t=T)
+            for i in range(BANKS):
+                there = slice((h % 2) * HALF + 2 * i, (h % 2) * HALF + 2 * i + 2)
+                nc.vector.tensor_tensor(
+                    out=qk[:, :, there, :].rearrange("p c j d -> p j c d"),
+                    in0=again_of[h][i][:, :, 0:QK].rearrange("p j (c d) -> p j c d", d=DK),
+                    in1=narrow[:, there, :].unsqueeze(3).to_broadcast([P, 2, CHUNKS, DK]),
+                    op=ALU.mult,
+                )
+            if h % 2 == 1:
+                pair = qk[:].rearrange("p c t d -> p (c t) d")[:, :, 0:2]
+                products = stage.tile([P, CHUNKS * T, 2, 2], F32, tag="products")
+                nc.gpsimd.tensor_tensor(
+                    out=products[:],
+                    in0=pair.unsqueeze(2).to_broadcast([P, CHUNKS * T, 2, 2]),
+                    in1=rotation_of["table"][:].rearrange("p w g r c -> p (w g) r c"),
+                    op=ALU.mult,
+                )
+                nc.gpsimd.tensor_add(
+                    out=pair, in0=products[:, :, :, 0], in1=products[:, :, :, 1]
+                )
+            for i in range(BANKS):
+                there = slice((h % 2) * HALF + 2 * i, (h % 2) * HALF + 2 * i + 2)
+                if i == 1 and h >= SHARE:
+                    for j in range(2):
+                        for head in range(H):
+                            t = there.start + j
+                            nc.scalar.activation(
+                                out=v_n[:, head, t, :],
+                                in_=again_of[h][i][:, j, QK + head * DV : QK + (head + 1) * DV],
+                                func=ACT.Copy,
+                                scale=wide[:, t, head : head + 1],
+                            )
+                    continue
+                nc.vector.tensor_tensor(
+                    out=v_n[:, :, there, :].rearrange("p h j d -> p j h d"),
+                    in0=again_of[h][i][:, :, QK:QKV].rearrange("p j (h d) -> p j h d", h=H),
+                    in1=wide[:, there, :].unsqueeze(3).to_broadcast([P, 2, H, DV]),
+                    op=ALU.mult,
+                )
+            if h % 2 == 1:
+                nc.sync.dma_start(
+                    out=rows_of(out_3, b), in_=v_n[:].rearrange("p h t d -> p h (t d)")
+                )
+                nc.sync.dma_start(
+                    out=rows_of(out_0, b),
+                    in_=qk[:, 0:H, :, :].rearrange("p h t d -> p h (t d)"),
+                )
+                nc.sync.dma_start(
+                    out=rows_of(out_2, b),
+                    in_=qk[:, H:CHUNKS, :, :].rearrange("p h t d -> p h (t d)"),
+                )
+
+        again_of = {}
+        rotation_of = {}
+        pools = {}
+
+        acc_banks = ctx.enter_context(tc.psum_pool(name="acc_banks", bufs=4))
+        with tc.psum_pool(name="flip_banks", bufs=4) as flip_banks:
+            pools["flip"] = flip_banks
             w_grouped = const.tile([P, COLS * PACK], BF16, align_bytes=64)
             w_words = w_grouped[:].bitcast(F32).rearrange("p (n u) -> p n u", u=2)
 
@@ -310,7 +382,7 @@ def tile_gatedscreeningtile_pa_t_kernel(
                 def flip_ahead():
                     if live(h + 4):
                         flipped_of[h + 4] = [
-                            flip(flip_banks, x_rows[h + 4], 2 * i, 2) for i in range(BANKS)
+                            flip(pools["flip"], x_rows[h + 4], 2 * i, 2) for i in range(BANKS)
                         ]
 
                 if h >= MMFIRST:
@@ -350,7 +422,7 @@ def tile_gatedscreeningtile_pa_t_kernel(
                         )
                     if h % 2 == 1:
                         fold(h // 2)
-                if h % 2 == 1 and live(h - SUM_LAG):
+                if h % 2 == SUM_LAG % 2 and live(h - SUM_LAG):
                     reduce((h - SUM_LAG) // 2)
                 for k in range(EARLY // 2):
                     if h == NEWTON_AT + 4 * k:
@@ -369,80 +441,35 @@ def tile_gatedscreeningtile_pa_t_kernel(
                             in_=gate[:].rearrange("p h t d -> p h (t d)"),
                         )
 
-            for h in range(-4, HALVES // 2):
+            for h in range(-4, HALVES - 3):
                 if h == TURNS_AT:
                     find_turns()
+                if h == TABLE_AT:
+                    rotation_of["table"] = finish_rotation_table()
                 first_sweep_step(h)
-            rotation = finish_rotation_table()
-            for h in range(HALVES // 2, HALVES + 1):
-                first_sweep_step(h)
+        again_banks = ctx.enter_context(tc.psum_pool(name="again_banks", bufs=4))
 
-        again_banks = ctx.enter_context(tc.psum_pool(name="again_banks", bufs=8))
+        def again(g):
+            again_of[g] = project(again_banks if g % 2 == 0 or g < ONLY else acc_banks, g)
+
+        for h in range(HALVES - 3, HALVES + 1):
+            for g in LATE.get(h, []) if GPOS == 0 else []:
+                again(g)
+            first_sweep_step(h)
+            for g in LATE.get(h, []):
+                if GPOS == 1:
+                    again(g)
+                scale(g)
+        done = sum(len(v) for v in LATE.values())
         AHEAD = 2
-        for h in range(AHEAD):
-            acc_of[h] = project(again_banks, h)
-        for h in range(HALVES):
-            b = h // 2
-            if h == LASTSUM:
+        for g in range(done, done + AHEAD):
+            again(g)
+        for g in range(done, HALVES):
+            if g == max(done, LASTSUM):
                 for k in range(SUMMED, B):
                     reduce(k)
                 clamp(EARLY, B)
                 invert(EARLY, B)
-            if live(h + AHEAD):
-                acc_of[h + AHEAD] = project(again_banks, h + AHEAD)
-            if h % 2 == 0:
-                qk = results.tile([P, CHUNKS, T, DK], F32, tag="qk")
-                v_n = results.tile([P, H, T, DV], F32, tag="v_n")
-            narrow = inverse[:, b, 0:NARROW].rearrange("p (t c) -> p t c", t=T)
-            wide = inverse[:, b, NARROW:].rearrange("p (t h) -> p t h", t=T)
-            for i in range(BANKS):
-                there = slice((h % 2) * HALF + 2 * i, (h % 2) * HALF + 2 * i + 2)
-                nc.vector.tensor_tensor(
-                    out=qk[:, :, there, :].rearrange("p c j d -> p j c d"),
-                    in0=acc_of[h][i][:, :, 0:QK].rearrange("p j (c d) -> p j c d", d=DK),
-                    in1=narrow[:, there, :].unsqueeze(3).to_broadcast([P, 2, CHUNKS, DK]),
-                    op=ALU.mult,
-                )
-            if h % 2 == 1:
-                pair = qk[:].rearrange("p c t d -> p (c t) d")[:, :, 0:2]
-                products = stage.tile([P, CHUNKS * T, 2, 2], F32, tag="products")
-                nc.gpsimd.tensor_tensor(
-                    out=products[:],
-                    in0=pair.unsqueeze(2).to_broadcast([P, CHUNKS * T, 2, 2]),
-                    in1=rotation[:].rearrange("p w g r c -> p (w g) r c"),
-                    op=ALU.mult,
-                )
-                nc.gpsimd.tensor_add(
-                    out=pair, in0=products[:, :, :, 0], in1=products[:, :, :, 1]
-                )
-            for i in range(BANKS):
-                there = slice((h % 2) * HALF + 2 * i, (h % 2) * HALF + 2 * i + 2)
-                if i == 1 and h >= SHARE:
-                    for j in range(2):
-                        for head in range(H):
-                            t = there.start + j
-                            nc.scalar.activation(
-                                out=v_n[:, head, t, :],
-                                in_=acc_of[h][i][:, j, QK + head * DV : QK + (head + 1) * DV],
-                                func=ACT.Copy,
-                                scale=wide[:, t, head : head + 1],
-                            )
-                    continue
-                nc.vector.tensor_tensor(
-                    out=v_n[:, :, there, :].rearrange("p h j d -> p j h d"),
-                    in0=acc_of[h][i][:, :, QK:QKV].rearrange("p j (h d) -> p j h d", h=H),
-                    in1=wide[:, there, :].unsqueeze(3).to_broadcast([P, 2, H, DV]),
-                    op=ALU.mult,
-                )
-            if h % 2 == 1:
-                nc.sync.dma_start(
-                    out=rows_of(out_3, b), in_=v_n[:].rearrange("p h t d -> p h (t d)")
-                )
-                nc.sync.dma_start(
-                    out=rows_of(out_0, b),
-                    in_=qk[:, 0:H, :, :].rearrange("p h t d -> p h (t d)"),
-                )
-                nc.sync.dma_start(
-                    out=rows_of(out_2, b),
-                    in_=qk[:, H:CHUNKS, :, :].rearrange("p h t d -> p h (t d)"),
-                )
+            if live(g + AHEAD):
+                again(g + AHEAD)
+            scale(g)

@@ -40,10 +40,12 @@ EARLY = 2
 GPOS = 1
 TABLE_AT = 8
 ONLY = 4
-LATE = {15: [0], 16: [1]}
+LATE = {16: [0, 1]}
 TURNS_AT = 1
 MMFIRST = -9
-NEWTON_AT = 6
+NEWTON_AT = {6: (0, 2)}
+CLAMP_AT = {5: (0, 2)}
+VFROM = 4
 SHARE = 4
 LASTSUM = 3
 SUM_LAG = 3
@@ -264,6 +266,12 @@ def tile_gatedscreeningtile_pa_t_kernel(
                 out=inverse[:, lo:hi, :], in_=sums[:, lo:hi, :], func=ACT.Abs_reciprocal_sqrt
             )
 
+        chain = []
+
+        def link():
+            if chain:
+                chain.pop(0)()
+
         def newton(lo, hi):
             shape = [P, hi - lo, NARROW + WIDE]
             s = sums[:, lo:hi, :]
@@ -278,6 +286,22 @@ def tile_gatedscreeningtile_pa_t_kernel(
                 t = const.tile(shape, F32, name="t%d_%d" % (k, lo))
                 better = const.tile(shape, F32, name="y%d_%d" % (k + 1, lo))
                 out = inverse[:, lo:hi, :] if k == 3 else better[:]
+                if k >= VFROM:
+                    chain.append(
+                        lambda t=t, y=y: nc.vector.tensor_tensor(out=t[:], in0=y, in1=y, op=ALU.mult)
+                    )
+                    chain.append(
+                        lambda t=t: nc.vector.scalar_tensor_tensor(
+                            out=t[:], in0=t[:], scalar=-0.5, in1=s, op0=ALU.mult, op1=ALU.mult
+                        )
+                    )
+                    chain.append(
+                        lambda t=t, y=y, out=out: nc.vector.scalar_tensor_tensor(
+                            out=out, in0=t[:], scalar=1.5, in1=y, op0=ALU.add, op1=ALU.mult
+                        )
+                    )
+                    y = out
+                    continue
                 nc.gpsimd.tensor_mul(out=t[:], in0=y, in1=y)
                 nc.gpsimd.tensor_mul(out=t[:], in0=t[:], in1=s)
                 nc.gpsimd.tensor_scalar(
@@ -393,6 +417,7 @@ def tile_gatedscreeningtile_pa_t_kernel(
                         in_=grouped_of[h + 1][:],
                     )
                     acc_of[h + 1] = project(acc_banks, h + 1)
+                    link()
                 if h < MMFIRST:
                     flip_ahead()
                 if live(h + 3):
@@ -422,13 +447,14 @@ def tile_gatedscreeningtile_pa_t_kernel(
                         )
                     if h % 2 == 1:
                         fold(h // 2)
+                link()
                 if h % 2 == SUM_LAG % 2 and live(h - SUM_LAG):
                     reduce((h - SUM_LAG) // 2)
-                for k in range(EARLY // 2):
-                    if h == NEWTON_AT + 4 * k:
-                        clamp(2 * k, 2 * k + 2)
-                    if h == NEWTON_AT + 4 * k + 1:
-                        newton(2 * k, 2 * k + 2)
+                link()
+                if h in CLAMP_AT:
+                    clamp(*CLAMP_AT[h])
+                if h in NEWTON_AT:
+                    newton(*NEWTON_AT[h])
                 if live(h - 1):
                     gate = gate_of[(h - 1) // 2]
                     there = slice(((h - 1) % 2) * HALF, ((h - 1) % 2 + 1) * HALF)
@@ -436,7 +462,7 @@ def tile_gatedscreeningtile_pa_t_kernel(
                         out=gate[:, :, there, :], in_=gate[:, :, there, :], func=ACT.Tanh
                     )
                     if (h - 1) % 2 == 1:
-                        nc.sync.dma_start(
+                        nc.scalar.dma_start(
                             out=rows_of(out_1, (h - 1) // 2),
                             in_=gate[:].rearrange("p h t d -> p h (t d)"),
                         )

import math
from contextlib import ExitStack

import concourse.mybir as mybir
from concourse.masks import make_identity

F32 = mybir.dt.float32
BF16 = mybir.dt.bfloat16
U32 = mybir.dt.uint32
U8 = mybir.dt.uint8
FP8X4 = mybir.dt.float8_e4m3fn_x4
ACT = mybir.ActivationFunctionType
ALU = mybir.AluOpType
AXIS = mybir.AxisListType

B, N, DIM, H, DK, DV = 8, 1024, 512, 2, 16, 48
HEAD = DK + DV
COLS = 2 * H * HEAD
CHUNKS = 2 * H
WT = 256.0
EPS = 1e-12
RSQRT_MAGIC = float(0x5F3759DF)

P = 128
PACK = 4
T = N // P
HALF = T // 2
HALVES = 2 * B
BANKS = HALF // 2
NARROW = T * CHUNKS
WIDE = T * H
QK = CHUNKS * DK
QKV = QK + H * DV

ROUND_MAGIC = 1.5 * 2.0**23
LOG_MAX = 6.0

FOLDS = 0
EARLY = 2
GPOS = 1
TABLE_AT = 8
ONLY = 4
LATE = {16: [0, 1]}
TURNS_AT = 1
MMFIRST = -9
NEWTON_AT = {6: (0, 2)}
CLAMP_AT = {5: (0, 2)}
VFROM = 4
SHARE = 4
LASTSUM = 3
SUM_LAG = 3
SUMMED = 7


def by_vector(h, i):
    return VPAT[h] > i


VPAT = [1, 1, 1, 2] + [1, 2, 1, 1] * 2 + [1, 1, 2, 2]

FLOPS = 2 * B * N * DIM * COLS


def tile_gatedscreeningtile_pa_t_kernel(
    tc, tokens, w_qg, w_kv, sm_log, out_0, out_1, out_2, out_3
):
    nc = tc.nc
    with ExitStack() as ctx:
        ctx.enter_context(tc.manual_schedule())
        const = ctx.enter_context(tc.tile_pool(name="const", bufs=1))
        resident = ctx.enter_context(tc.tile_pool(name="resident", bufs=1))
        stage = ctx.enter_context(tc.tile_pool(name="stage", bufs=3))
        results = ctx.enter_context(tc.tile_pool(name="results", bufs=8))
        deep = ctx.enter_context(tc.tile_pool(name="deep", bufs=4))

        def live(h):
            return 0 <= h < HALVES

        def rows_of(dram, b):
            return dram[b].rearrange("h (p t) d -> p h (t d)", t=T)

        log_window = const.tile([P, H], BF16)
        nc.scalar.dma_start(out=log_window[:], in_=sm_log.partition_broadcast(P))
        w_rows = const.tile([P, 2, DIM], BF16)
        nc.sync.dma_start(out=w_rows[:, 0, :], in_=w_qg)
        nc.sync.dma_start(out=w_rows[:, 1, :], in_=w_kv)
        x_rows = []
        for h in range(HALVES):
            x_h = resident.tile([P, HALF, DIM], BF16, name="x_rows%d" % h)
            first = (h % 2) * HALF
            rows = tokens[h // 2].rearrange("(p t) k -> p t k", t=T)[:, first : first + HALF, :]
            for part in (slice(0, 2), slice(2, 4)) if h == 0 else (slice(0, HALF),):
                nc.sync.dma_start(out=x_h[:, part, :], in_=rows[:, part, :])
            x_rows.append(x_h)

        warm = const.tile([P, 1], F32)
        nc.vector.memset(warm[:], 0.0)
        nc.scalar.activation(out=warm[:], in_=warm[:], func=ACT.Silu)

        ident = const.tile([P, P], F32)
        make_identity(nc, ident[:])

        two = const.tile([P, H], F32)
        minus_one = const.tile([P, H], F32)
        position = const.tile([P, T], F32)
        window = const.tile([P, H], F32)
        nc.gpsimd.memset(two[:], 2.0)
        nc.gpsimd.memset(minus_one[:], -1.0)
        nc.gpsimd.iota(
            position[:], pattern=[[1, T]], base=0, channel_multiplier=T,
            allow_small_or_imprecise_dtypes=True,
        )
        nc.gpsimd.tensor_scalar(
            out=window[:], in0=log_window[:], scalar1=LOG_MAX, scalar2=1.0 / math.log(2.0),
            op0=ALU.min, op1=ALU.mult,
        )
        nc.gpsimd.tensor_tensor(out=window[:], in0=two[:], in1=window[:], op=ALU.pow)
        nc.gpsimd.tensor_scalar(
            out=window[:], in0=window[:], scalar1=1.0, scalar2=WT, op0=ALU.add, op1=ALU.min
        )
        cos_window = const.tile([P, H], F32)
        per_position = const.tile([P, H], F32)
        turns = const.tile([P, H, T], F32)
        whole = const.tile([P, H, T], F32)

        def find_turns():
            nc.scalar.activation(
                out=cos_window[:], in_=window[:], func=ACT.Sin, scale=-math.pi / WT, bias=math.pi / 2
            )
            nc.gpsimd.tensor_tensor(out=per_position[:], in0=window[:], in1=minus_one[:], op=ALU.pow)
            nc.gpsimd.tensor_scalar_add(out=cos_window[:], in0=cos_window[:], scalar1=1.0)
            nc.gpsimd.tensor_mul(out=per_position[:], in0=per_position[:], in1=cos_window[:])
            for head in range(H):
                nc.gpsimd.tensor_scalar(
                    out=turns[:, head, :], in0=position[:],
                    scalar1=per_position[:, head : head + 1], scalar2=0.25,
                    op0=ALU.mult, op1=ALU.mult,
                )
            nc.gpsimd.tensor_scalar(
                out=whole[:], in0=turns[:], scalar1=ROUND_MAGIC, scalar2=ROUND_MAGIC,
                op0=ALU.add, op1=ALU.subtract,
            )
            nc.gpsimd.tensor_sub(out=turns[:], in0=turns[:], in1=whole[:])

        def finish_rotation_table():
            sin_half = const.tile([P, H * T], F32)
            sin_quarter = const.tile([P, H * T], F32)
            flat_turns = turns[:].rearrange("p h t -> p (h t)")
            nc.scalar.activation(out=sin_half[:], in_=flat_turns, func=ACT.Sin, scale=math.pi)
            nc.scalar.activation(
                out=sin_quarter[:], in_=flat_turns, func=ACT.Sin, scale=math.pi / 2
            )
            cos_half = const.tile([P, H * T], F32)
            nc.gpsimd.tensor_mul(out=cos_half[:], in0=sin_quarter[:], in1=sin_quarter[:])
            nc.gpsimd.tensor_scalar(
                out=cos_half[:], in0=cos_half[:], scalar1=-2.0, scalar2=1.0,
                op0=ALU.mult, op1=ALU.add,
            )
            half_sin_x = const.tile([P, H * T], F32)
            nc.gpsimd.tensor_mul(out=half_sin_x[:], in0=sin_half[:], in1=cos_half[:])
            sin_half_squared = const.tile([P, H * T], F32)
            nc.gpsimd.tensor_mul(out=sin_half_squared[:], in0=sin_half[:], in1=sin_half[:])
            table = const.tile([P, 2, H * T, 2, 2], F32, name="rotation")
            for_q_and_k = [P, 2, H * T]
            for diagonal in range(2):
                nc.gpsimd.tensor_scalar(
                    out=table[:, :, :, diagonal, diagonal],
                    in0=sin_half_squared[:].unsqueeze(1).to_broadcast(for_q_and_k),
                    scalar1=-2.0, scalar2=1.0, op0=ALU.mult, op1=ALU.add,
                )
            nc.gpsimd.tensor_scalar_mul(
                out=table[:, :, :, 0, 1],
                in0=half_sin_x[:].unsqueeze(1).to_broadcast(for_q_and_k), scalar1=-2.0,
            )
            nc.gpsimd.tensor_scalar_mul(
                out=table[:, :, :, 1, 0],
                in0=half_sin_x[:].unsqueeze(1).to_broadcast(for_q_and_k), scalar1=2.0,
            )
            return table

        def flip(banks, rows, first, count):
            words = rows[:].bitcast(F32)
            flipped = banks.tile([P, 2, 2, P], F32, tag="flipped")
            for j in range(count):
                for u in range(2):
                    nc.tensor.transpose(
                        flipped[:, j, u, :], words[:, first + j, u : 2 * P : 2], ident[:]
                    )
            return flipped

        def regroup(copy, flipped, grouped):
            copy(
                out=grouped.bitcast(F32).rearrange("p (j r u) -> p j r u", j=2, u=2),
                in_=flipped[:].rearrange("p j u r -> p j r u"),
            )

        BANK_COLS = 2 * P * PACK
        w_codes = const.tile([P, COLS], U32, align_bytes=64)
        w_scales = const.tile([P, COLS], U8, align_bytes=64)
        x_codes = []
        x_scales = []
        for h in range(HALVES):
            x_codes.append(resident.tile([P, HALF * P], U32, name="x_codes%d" % h, align_bytes=64))
            x_scales.append(resident.tile([P, HALF * P], U8, name="x_scales%d" % h, align_bytes=64))

        def project(banks, h):
            products = []
            for i in range(BANKS):
                acc = banks.tile([P, 2, COLS], F32, tag="acc")
                for j in range(2):
                    cols = slice((2 * i + j) * P, (2 * i + j + 1) * P)
                    nc.tensor.matmul_mx(
                        out=acc[:, j, :],
                        lhsT=x_codes[h][:, cols].bitcast(FP8X4),
                        lhsT_scale=x_scales[h][:, cols],
                        rhs=w_codes[:].bitcast(FP8X4),
                        rhs_scale=w_scales[:],
                        start=True,
                        stop=True,
                    )
                products.append(acc)
            return products

        sums = const.tile([P, B, NARROW + WIDE], F32)
        inverse = const.tile([P, B, NARROW + WIDE], F32)
        flipped_of = {}
        grouped_of = {}
        acc_of = {}
        squares_of = {}
        folded_of = {}
        gate_of = {}

        def fold(b):
            sq = squares_of[b]
            q = sq[:, :, 0:QK].rearrange("p t (c d) -> p t c d", d=DK)
            v = sq[:, :, QK:].rearrange("p t (h d) -> p t h d", h=H)
            for level in range(FOLDS):
                dk = DK // 2 ** (level + 1)
                dv = DV // 2 ** (level + 1)
                less_v = stage.tile([P, T, H, dv], F32, name="less_v%d" % level, tag="less_v%d" % level)
                less_q = stage.tile([P, T, CHUNKS, dk], F32, name="less_q%d" % level, tag="less_q%d" % level)
                nc.gpsimd.tensor_add(out=less_v[:], in0=v[:, :, :, 0:dv], in1=v[:, :, :, dv : 2 * dv])
                nc.gpsimd.tensor_add(out=less_q[:], in0=q[:, :, :, 0:dk], in1=q[:, :, :, dk : 2 * dk])
                v = less_v[:]
                q = less_q[:]
            folded_of[b] = (q, v)

        def reduce(b):
            q, v = folded_of[b]
            nc.vector.tensor_reduce(
                out=sums[:, b, 0:NARROW].rearrange("p (t c) -> p t c", t=T), in_=q,
                axis=AXIS.X, op=ALU.add,
            )
            nc.vector.tensor_reduce(
                out=sums[:, b, NARROW:].rearrange("p (t h) -> p t h", t=T), in_=v,
                axis=AXIS.X, op=ALU.add,
            )

        def clamp(lo, hi):
            nc.vector.tensor_scalar_max(
                out=sums[:, lo:hi, :], in0=sums[:, lo:hi, :], scalar1=EPS * EPS
            )

        def invert(lo, hi):
            nc.scalar.activation(
                out=inverse[:, lo:hi, :], in_=sums[:, lo:hi, :], func=ACT.Abs_reciprocal_sqrt
            )

        chain = []

        def link():
            if chain:
                chain.pop(0)()

        def newton(lo, hi):
            shape = [P, hi - lo, NARROW + WIDE]
            s = sums[:, lo:hi, :]
            guess = const.tile(shape, U32, name="guess%d" % lo)
            y = const.tile(shape, F32, name="y0_%d" % lo)
            nc.scalar.activation(
                out=guess[:], in_=s.bitcast(U32), func=ACT.Identity, scale=-0.5, bias=RSQRT_MAGIC
            )
            nc.scalar.copy(out=y[:], in_=guess[:].bitcast(F32))
            y = y[:]
            for k in range(4):
                t = const.tile(shape, F32, name="t%d_%d" % (k, lo))
                better = const.tile(shape, F32, name="y%d_%d" % (k + 1, lo))
                out = inverse[:, lo:hi, :] if k == 3 else better[:]
                if k >= VFROM:
                    chain.append(
                        lambda t=t, y=y: nc.vector.tensor_tensor(out=t[:], in0=y, in1=y, op=ALU.mult)
                    )
                    chain.append(
                        lambda t=t: nc.vector.scalar_tensor_tensor(
                            out=t[:], in0=t[:], scalar=-0.5, in1=s, op0=ALU.mult, op1=ALU.mult
                        )
                    )
                    chain.append(
                        lambda t=t, y=y, out=out: nc.vector.scalar_tensor_tensor(
                            out=out, in0=t[:], scalar=1.5, in1=y, op0=ALU.add, op1=ALU.mult
                        )
                    )
                    y = out
                    continue
                nc.gpsimd.tensor_mul(out=t[:], in0=y, in1=y)
                nc.gpsimd.tensor_mul(out=t[:], in0=t[:], in1=s)
                nc.gpsimd.tensor_scalar(
                    out=t[:], in0=t[:], scalar1=-0.5, scalar2=1.5, op0=ALU.mult, op1=ALU.add
                )
                nc.gpsimd.tensor_mul(out=out, in0=y, in1=t[:])
                y = out

        out_of = {}

        def scale(h):
            b = h // 2
            if h % 2 == 0:
                out_of[b] = (
                    results.tile([P, CHUNKS, T, DK], F32, name="qk", tag="qk"),
                    results.tile([P, H, T, DV], F32, name="v_n", tag="v_n"),
                )
            qk, v_n = out_of[b]
            narrow = inverse[:, b, 0:NARROW].rearrange("p (t c) -> p t c", t=T)
            wide = inverse[:, b, NARROW:].rearrange("p (t h) -> p t h", t=T)
            for i in range(BANKS):
                there = slice((h % 2) * HALF + 2 * i, (h % 2) * HALF + 2 * i + 2)
                nc.vector.tensor_tensor(
                    out=qk[:, :, there, :].rearrange("p c j d -> p j c d"),
                    in0=again_of[h][i][:, :, 0:QK].rearrange("p j (c d) -> p j c d", d=DK),
                    in1=narrow[:, there, :].unsqueeze(3).to_broadcast([P, 2, CHUNKS, DK]),
                    op=ALU.mult,
                )
            if h % 2 == 1:
                pair = qk[:].rearrange("p c t d -> p (c t) d")[:, :, 0:2]
                products = stage.tile([P, CHUNKS * T, 2, 2], F32, tag="products")
                nc.gpsimd.tensor_tensor(
                    out=products[:],
                    in0=pair.unsqueeze(2).to_broadcast([P, CHUNKS * T, 2, 2]),
                    in1=rotation_of["table"][:].rearrange("p w g r c -> p (w g) r c"),
                    op=ALU.mult,
                )
                nc.gpsimd.tensor_add(
                    out=pair, in0=products[:, :, :, 0], in1=products[:, :, :, 1]
                )
            for i in range(BANKS):
                there = slice((h % 2) * HALF + 2 * i, (h % 2) * HALF + 2 * i + 2)
                if i == 1 and h >= SHARE:
                    for j in range(2):
                        for head in range(H):
                            t = there.start + j
                            nc.scalar.activation(
                                out=v_n[:, head, t, :],
                                in_=again_of[h][i][:, j, QK + head * DV : QK + (head + 1) * DV],
                                func=ACT.Copy,
                                scale=wide[:, t, head : head + 1],
                            )
                    continue
                nc.vector.tensor_tensor(
                    out=v_n[:, :, there, :].rearrange("p h j d -> p j h d"),
                    in0=again_of[h][i][:, :, QK:QKV].rearrange("p j (h d) -> p j h d", h=H),
                    in1=wide[:, there, :].unsqueeze(3).to_broadcast([P, 2, H, DV]),
                    op=ALU.mult,
                )
            if h % 2 == 1:
                nc.sync.dma_start(
                    out=rows_of(out_3, b), in_=v_n[:].rearrange("p h t d -> p h (t d)")
                )
                nc.sync.dma_start(
                    out=rows_of(out_0, b),
                    in_=qk[:, 0:H, :, :].rearrange("p h t d -> p h (t d)"),
                )
                nc.sync.dma_start(
                    out=rows_of(out_2, b),
                    in_=qk[:, H:CHUNKS, :, :].rearrange("p h t d -> p h (t d)"),
                )

        again_of = {}
        rotation_of = {}
        pools = {}

        acc_banks = ctx.enter_context(tc.psum_pool(name="acc_banks", bufs=4))
        with tc.psum_pool(name="flip_banks", bufs=4) as flip_banks:
            pools["flip"] = flip_banks
            w_grouped = const.tile([P, COLS * PACK], BF16, align_bytes=64)
            w_words = w_grouped[:].bitcast(F32).rearrange("p (n u) -> p n u", u=2)

            def place(copy, flipped, lo, hi, first):
                copy(
                    out=w_words[:, first : first + H * (hi - lo), :].rearrange(
                        "p (h d) u -> p h d u", h=H
                    ),
                    in_=flipped[:, 0, :, :].rearrange("p u (h d) -> p h d u", h=H)[:, :, lo:hi, :],
                )

            qg_flipped = flip(flip_banks, w_rows, 0, 1)
            kv_flipped = flip(flip_banks, w_rows, 1, 1)
            place(nc.vector.tensor_copy, qg_flipped, 0, DK, 0)
            place(nc.scalar.copy, kv_flipped, 0, DK, H * DK)
            place(nc.scalar.copy, kv_flipped, DK, HEAD, QK)
            place(nc.vector.tensor_copy, qg_flipped, DK, HEAD, QKV)
            nc.vector.quantize_mx(
                out=w_codes[:].bitcast(FP8X4), scales=w_scales[:], in_=w_grouped[:]
            )

            def first_sweep_step(h):
                def flip_ahead():
                    if live(h + 4):
                        flipped_of[h + 4] = [
                            flip(pools["flip"], x_rows[h + 4], 2 * i, 2) for i in range(BANKS)
                        ]

                if h >= MMFIRST:
                    flip_ahead()
                if live(h + 1):
                    nc.vector.quantize_mx(
                        out=x_codes[h + 1][:].bitcast(FP8X4), scales=x_scales[h + 1][:],
                        in_=grouped_of[h + 1][:],
                    )
                    acc_of[h + 1] = project(acc_banks, h + 1)
                    link()
                if h < MMFIRST:
                    flip_ahead()
                if live(h + 3):
                    grouped = deep.tile([P, BANKS * BANK_COLS], BF16, tag="grouped", align_bytes=64)
                    grouped_of[h + 3] = grouped
                    for i in range(BANKS):
                        copy = nc.vector.tensor_copy if by_vector(h + 3, i) else nc.scalar.copy
                        regroup(
                            copy, flipped_of[h + 3][i],
                            grouped[:, i * BANK_COLS : (i + 1) * BANK_COLS],
                        )
                if live(h):
                    if h % 2 == 0:
                        gate_of[h // 2] = results.tile([P, H, T, DV], F32, name="gate", tag="gate")
                        squares_of[h // 2] = stage.tile([P, T, QKV], F32, name="sq", tag="sq")
                    for i in range(BANKS):
                        acc = acc_of[h][i]
                        there = slice((h % 2) * HALF + 2 * i, (h % 2) * HALF + 2 * i + 2)
                        nc.scalar.activation(
                            out=squares_of[h // 2][:, there, :], in_=acc[:, :, 0:QKV],
                            func=ACT.Square,
                        )
                        nc.scalar.activation(
                            out=gate_of[h // 2][:, :, there, :].rearrange("p h j d -> p j h d"),
                            in_=acc[:, :, QKV:].rearrange("p j (h d) -> p j h d", h=H),
                            func=ACT.Silu,
                        )
                    if h % 2 == 1:
                        fold(h // 2)
                link()
                if h % 2 == SUM_LAG % 2 and live(h - SUM_LAG):
                    reduce((h - SUM_LAG) // 2)
                link()
                if h in CLAMP_AT:
                    clamp(*CLAMP_AT[h])
                if h in NEWTON_AT:
                    newton(*NEWTON_AT[h])
                if live(h - 1):
                    gate = gate_of[(h - 1) // 2]
                    there = slice(((h - 1) % 2) * HALF, ((h - 1) % 2 + 1) * HALF)
                    nc.scalar.activation(
                        out=gate[:, :, there, :], in_=gate[:, :, there, :], func=ACT.Tanh
                    )
                    if (h - 1) % 2 == 1:
                        nc.scalar.dma_start(
                            out=rows_of(out_1, (h - 1) // 2),
                            in_=gate[:].rearrange("p h t d -> p h (t d)"),
                        )

            for h in range(-4, HALVES - 3):
                if h == TURNS_AT:
                    find_turns()
                if h == TABLE_AT:
                    rotation_of["table"] = finish_rotation_table()
                first_sweep_step(h)
        again_banks = ctx.enter_context(tc.psum_pool(name="again_banks", bufs=4))

        def again(g):
            again_of[g] = project(again_banks if g % 2 == 0 or g < ONLY else acc_banks, g)

        for h in range(HALVES - 3, HALVES + 1):
            for g in LATE.get(h, []) if GPOS == 0 else []:
                again(g)
            first_sweep_step(h)
            for g in LATE.get(h, []):
                if GPOS == 1:
                    again(g)
                scale(g)
        done = sum(len(v) for v in LATE.values())
        AHEAD = 2
        for g in range(done, done + AHEAD):
            again(g)
        for g in range(done, HALVES):
            if g == max(done, LASTSUM):
                for k in range(SUMMED, B):
                    reduce(k)
                clamp(EARLY, B)
                invert(EARLY, B)
            if live(g + AHEAD):
                again(g + AHEAD)
            scale(g)
